import numpy as np
import ml_dtypes


def mxq(x, axis, fmt="e4m3"):
    dtype, down = {"e4m3": (ml_dtypes.float8_e4m3fn, 7), "e5m2": (ml_dtypes.float8_e5m2, 14)}[fmt]
    v = np.moveaxis(np.asarray(x, np.float32).astype(ml_dtypes.bfloat16).astype(np.float64), axis, -1)
    blocks = v.reshape(v.shape[:-1] + (-1, 32))
    amax = np.abs(blocks).max(-1, keepdims=True)
    byte = np.maximum(np.where(amax > 0, np.frexp(amax)[1] - 1 + 127, 0) - down, 1)
    scale = np.exp2(byte - 127.0)
    codes = (blocks / scale).astype(np.float32).astype(dtype).astype(np.float64)
    return np.moveaxis((codes * scale).reshape(v.shape), -1, axis)


WIDE = False


def mx_kscale(k):
    if not WIDE:
        return np.ones(k)
    levels = np.array([10, -10, 5, -5, 0])
    if k % 512:
        return np.exp2(np.random.permutation(np.resize(levels, k // 32))).repeat(32)
    a = np.empty((k // 512, 16))
    for p in range(k // 512):
        a[p, :8] = np.random.permutation(np.resize(levels, 8))
        for g in range(8):
            far = levels[np.abs(levels - a[p, g]) >= 10]
            a[p, g + 8] = far[np.random.randint(len(far))]
    return np.exp2(a.ravel()).repeat(32)


BF16 = ml_dtypes.bfloat16


def bf(x):
    return np.asarray(x, np.float32).astype(BF16)


def f64(x):
    return np.asarray(x).astype(np.float64)


B, R, U, HID, G = 1024, 1024, 512, 1024, 1024


def sigmoid(v):
    return 1.0 / (1.0 + np.exp(-v))


def setup_inputs():
    s = mx_kscale(R)
    return {"y_tilde": bf(np.random.standard_normal((B, R)) * s),
            "z_next": bf(np.random.standard_normal((B, R)) * s),
            "dt": bf(0.3 + 0.2 * np.random.random(1)),
            "glu_w1": bf(np.random.standard_normal((G, R)) * 1.5 / np.sqrt(R) / s),
            "glu_w2": bf(np.random.standard_normal((G, R)) / np.sqrt(R) / s),
            "glu_b1": bf(np.random.standard_normal(G) * 0.3),
            "glu_b2": bf(np.random.standard_normal(G) * 0.3)}


def reference(y_tilde, z_next, dt, glu_w1, glu_w2, glu_b1, glu_b2):
    y_next = f64(y_tilde) + f64(dt) * f64(z_next)
    yq = mxq(y_next, 1, "e4m3")
    gate = sigmoid((yq @ mxq(f64(glu_w1), 1, "e4m3").T) + f64(glu_b1))
    return gate * ((yq @ mxq(f64(glu_w2), 1, "e4m3").T) + f64(glu_b2))

@@ -1,0 +1,299 @@
+from contextlib import ExitStack
+
+import concourse.mybir as mybir
+from concourse.masks import make_identity
+
+F32 = mybir.dt.float32
+BF16 = mybir.dt.bfloat16
+U32 = mybir.dt.uint32
+U8 = mybir.dt.uint8
+FP8X4 = mybir.dt.float8_e4m3fn_x4
+ALU = mybir.AluOpType
+ACT = mybir.ActivationFunctionType
+
+P = 128
+ROWS = 1024
+K = 1024
+UNITS = 1024
+PACK = 4
+K_PASS = P * PACK
+PASSES = K // K_PASS
+BANK = 512
+ROW_TILES = ROWS // P
+UNIT_TILES = UNITS // P
+FIRST_TILES = BANK // P
+STORE_TILES = 2
+
+FLOPS = 2 * 2 * ROWS * K * UNITS
+
+
+def tile_instrumentedlocmblock_pb_kernel(
+    tc, y_tilde, z_next, dt, glu_w1, glu_w2, glu_b1, glu_b2, out
+):
+    nc = tc.nc
+    with ExitStack() as ctx:
+        ctx.enter_context(tc.manual_schedule())
+        keep = ctx.enter_context(tc.tile_pool(name="keep", bufs=1))
+        rows_pool = ctx.enter_context(tc.tile_pool(name="rows", bufs=4))
+        grouped_pool = ctx.enter_context(tc.tile_pool(name="grouped", bufs=4))
+        gated_pool = ctx.enter_context(tc.tile_pool(name="gated", bufs=3))
+        acc_pool = ctx.enter_context(tc.psum_pool(name="acc", bufs=2))
+        flip_pool = ctx.enter_context(tc.psum_pool(name="flip", bufs=4))
+
+        dt_bf16 = keep.tile([P, 1], BF16)
+        nc.scalar.dma_start(out=dt_bf16[:], in_=dt.partition_broadcast(P))
+
+        bias_rows = keep.tile([P, P], BF16)
+        nc.vector.memset(bias_rows[:], 0.0)
+        nc.scalar.dma_start(
+            out=bias_rows[0:UNIT_TILES, :], in_=glu_b1.rearrange("(g p) -> g p", p=P)
+        )
+        nc.scalar.dma_start(
+            out=bias_rows[UNIT_TILES : 2 * UNIT_TILES, :],
+            in_=glu_b2.rearrange("(g p) -> g p", p=P),
+        )
+
+        zero_col = keep.tile([P, 1], F32)
+        nc.vector.memset(zero_col[:], 0.0)
+        table_warm = keep.tile([P, 1], F32)
+        nc.scalar.activation(out=table_warm[:], in_=zero_col[:], func=ACT.Sigmoid)
+
+        dt_f32 = keep.tile([P, 1], F32)
+        nc.vector.tensor_copy(out=dt_f32[:], in_=dt_bf16[:])
+
+        ident_bf16 = keep.tile([P, P], BF16)
+        make_identity(nc, ident_bf16[:])
+        ident_f32 = keep.tile([P, P], F32)
+        make_identity(nc, ident_f32[:])
+
+        y_view = y_tilde.rearrange("(p t) k -> p t k", t=ROW_TILES)
+        z_view = z_next.rearrange("(p t) k -> p t k", t=ROW_TILES)
+        out_view = out.rearrange("(p t) g -> p t g", t=ROW_TILES)
+        y_raw = keep.tile([P, ROW_TILES, K], BF16)
+        z_raw = keep.tile([P, ROW_TILES, K], BF16)
+
+        def load_rows(t):
+            nc.sync.dma_start(out=y_raw[:, t, :], in_=y_view[:, t, :])
+            nc.sync.dma_start(out=z_raw[:, t, :], in_=z_view[:, t, :])
+
+        for t in range(FIRST_TILES):
+            load_rows(t)
+        weights = (glu_w1, glu_w2)
+        w_raw = {}
+        for g in range(UNIT_TILES):
+            for w in range(2):
+                w_raw[w, g] = keep.tile([P, K], BF16, name="w_raw_%d_%d" % (w, g))
+                nc.sync.dma_start(out=w_raw[w, g][:], in_=weights[w][g * P : (g + 1) * P, :])
+            if g % 2 == 0:
+                load_rows(FIRST_TILES + g // 2)
+        bias_all = keep.tile([P, 2, UNITS], BF16)
+        nc.sync.dma_start(out=bias_all[:, 0, :], in_=glu_b1.partition_broadcast(P))
+        nc.sync.dma_start(out=bias_all[:, 1, :], in_=glu_b2.partition_broadcast(P))
+
+        y_codes = keep.tile([P, PASSES, ROWS], U32, align_bytes=64)
+        y_scales = keep.tile([P, PASSES, ROWS], U8, align_bytes=64)
+        w_codes = keep.tile([P, 2, PASSES, UNITS], U32, align_bytes=64)
+        w_scales = keep.tile([P, 2, PASSES, UNITS], U8, align_bytes=64)
+        bias_cols = keep.tile([P, 2 * UNIT_TILES], F32)
+        out_rows = keep.tile([P, ROW_TILES, UNITS], F32)
+
+        y_next = {}
+        y_grouped = {}
+        w_grouped = {}
+        acc = {}
+        gate = {}
+        gated = {}
+        flipped_out = {}
+
+        def regroup(source, grouped, passes):
+            words = source.bitcast(F32)
+            flipped = flip_pool.tile([P, passes * 2, P], F32, name="flipped", tag="flipped")
+            for s in range(passes):
+                for u in range(2):
+                    nc.tensor.transpose(
+                        flipped[:, 2 * s + u, :],
+                        words[:, 2 * P * s + u : 2 * P * (s + 1) : 2],
+                        ident_f32[:],
+                    )
+            nc.scalar.copy(
+                out=grouped.bitcast(F32).rearrange("p (s r u) -> p s r u", s=passes, u=2),
+                in_=flipped[:].rearrange("p (s u) r -> p s r u", u=2),
+            )
+
+        def quantise(grouped, codes, scales, first, count, cols):
+            for i in range(count):
+                nc.vector.quantize_mx(
+                    out=codes[:, first + i, cols].bitcast(FP8X4),
+                    scales=scales[:, first + i, cols],
+                    in_=grouped[:, i * K_PASS : (i + 1) * K_PASS],
+                )
+
+        def update_rows(t, first, count):
+            ks = slice(first * K_PASS, (first + count) * K_PASS)
+            y_next[t, first] = rows_pool.tile([P, count * K_PASS], BF16, name="y_next", tag="y_next")
+            nc.vector.scalar_tensor_tensor(
+                out=y_next[t, first][:],
+                in0=z_raw[:, t, ks],
+                scalar=dt_f32[:, 0:1],
+                in1=y_raw[:, t, ks],
+                op0=ALU.mult,
+                op1=ALU.add,
+            )
+
+        def transpose_rows(t, first, count):
+            y_grouped[t, first] = grouped_pool.tile(
+                [P, count * K_PASS], BF16, name="y_grouped", tag="y_grouped", align_bytes=64
+            )
+            regroup(y_next[t, first][:], y_grouped[t, first][:], count)
+
+        def quantise_rows(t, first, count):
+            quantise(y_grouped[t, first], y_codes, y_scales, first, count, slice(t * P, (t + 1) * P))
+
+        def transpose_weights(g):
+            for w in range(2):
+                w_grouped[w, g] = grouped_pool.tile(
+                    [P, K], BF16, name="w_grouped", tag="w_grouped", align_bytes=64
+                )
+                regroup(w_raw[w, g][:], w_grouped[w, g][:], PASSES)
+
+        def quantise_weights(g):
+            for w in range(2):
+                quantise(
+                    w_grouped[w, g],
+                    w_codes[:, w, :, :],
+                    w_scales[:, w, :, :],
+                    0,
+                    PASSES,
+                    slice(g * P, (g + 1) * P),
+                )
+
+        def rows_operand(rows):
+            return lambda w, s: (y_codes[:, s, rows], y_scales[:, s, rows])
+
+        def units_operand(units):
+            return lambda w, s: (w_codes[:, w, s, units], w_scales[:, w, s, units])
+
+        def multiply(stationary, moving):
+            sums = []
+            for w in range(2):
+                total = acc_pool.tile([P, BANK], F32, name="acc_%d" % w, tag="acc_%d" % w)
+                for s in range(PASSES):
+                    lhs_codes, lhs_scales = stationary(w, s)
+                    rhs_codes, rhs_scales = moving(w, s)
+                    nc.tensor.matmul_mx(
+                        out=total[:],
+                        lhsT=lhs_codes.bitcast(FP8X4),
+                        lhsT_scale=lhs_scales,
+                        rhs=rhs_codes.bitcast(FP8X4),
+                        rhs_scale=rhs_scales,
+                        start=(s == 0),
+                        stop=(s == PASSES - 1),
+                    )
+                sums.append(total)
+            return sums
+
+        def multiply_units(g):
+            acc[g] = multiply(units_operand(slice(g * P, (g + 1) * P)), rows_operand(slice(0, BANK)))
+
+        def open_gate(g):
+            gate[g] = gated_pool.tile([P, BANK], F32, name="gate", tag="gate")
+            nc.scalar.activation(
+                out=gate[g][:],
+                in_=acc[g][0][:],
+                func=ACT.Sigmoid,
+                bias=bias_cols[:, g : g + 1],
+                scale=1.0,
+            )
+
+        def apply_gate(g):
+            gated[g] = gated_pool.tile([P, BANK], F32, name="gated", tag="gated")
+            nc.vector.scalar_tensor_tensor(
+                out=gated[g][:],
+                in0=acc[g][1][:],
+                scalar=bias_cols[:, UNIT_TILES + g : UNIT_TILES + g + 1],
+                in1=gate[g][:],
+                op0=ALU.add,
+                op1=ALU.mult,
+            )
+
+        def transpose_out(g):
+            flipped_out[g] = flip_pool.tile([P, FIRST_TILES, P], F32, name="flipped", tag="flipped")
+            for t in range(FIRST_TILES):
+                nc.tensor.transpose(
+                    flipped_out[g][:, t, :], gated[g][:, t * P : (t + 1) * P], ident_f32[:]
+                )
+
+        def copy_out(g):
+            copy = nc.vector.tensor_copy if g % 2 == 0 else nc.scalar.copy
+            copy(out=out_rows[:, 0:FIRST_TILES, g * P : (g + 1) * P], in_=flipped_out[g][:])
+            if g % STORE_TILES == STORE_TILES - 1:
+                units = slice((g + 1 - STORE_TILES) * P, (g + 1) * P)
+                nc.sync.dma_start(
+                    out=out_view[:, 0:FIRST_TILES, units], in_=out_rows[:, 0:FIRST_TILES, units]
+                )
+
+        def rows_step(t, half):
+            units = slice(half * BANK, (half + 1) * BANK)
+            sums = multiply(rows_operand(slice(t * P, (t + 1) * P)), units_operand(units))
+            biased = []
+            for w in range(2):
+                biased.append(gated_pool.tile([P, BANK], F32, name="biased_%d" % w, tag="biased_%d" % w))
+                nc.vector.tensor_tensor(
+                    out=biased[w][:], in0=sums[w][:], in1=bias_all[:, w, units], op=ALU.add
+                )
+            gate_rows = gated_pool.tile([P, BANK], F32, name="gate", tag="gate")
+            nc.scalar.activation(out=gate_rows[:], in_=biased[0][:], func=ACT.Sigmoid)
+            nc.gpsimd.tensor_tensor(
+                out=out_rows[:, t, units], in0=gate_rows[:], in1=biased[1][:], op=ALU.mult
+            )
+            nc.sync.dma_start(out=out_view[:, t, units], in_=out_rows[:, t, units])
+
+        update_rows(0, 0, PASSES)
+        for t in range(FIRST_TILES):
+            if t + 1 < FIRST_TILES:
+                update_rows(t + 1, 0, PASSES)
+            transpose_rows(t, 0, PASSES)
+        for t in range(FIRST_TILES):
+            quantise_rows(t, 0, PASSES)
+
+        LATER = (ROW_TILES - FIRST_TILES) * PASSES
+
+        def later_piece(j):
+            t, first = divmod(j, PASSES)
+            return FIRST_TILES + t, first, 1
+
+        update_rows(*later_piece(0))
+        transpose_weights(0)
+        quantise_weights(0)
+
+        bias_flipped = flip_pool.tile([P, P], BF16, name="flipped", tag="flipped")
+        nc.tensor.transpose(bias_flipped[:], bias_rows[:], ident_bf16[:])
+        nc.vector.tensor_copy(out=bias_cols[:], in_=bias_flipped[:, 0 : 2 * UNIT_TILES])
+
+        transpose_weights(1)
+        transpose_rows(*later_piece(0))
+
+        for g in range(UNIT_TILES):
+            multiply_units(g)
+            open_gate(g)
+            if g + 1 < LATER:
+                update_rows(*later_piece(g + 1))
+            if g + 1 < UNIT_TILES:
+                quantise_weights(g + 1)
+            quantise_rows(*later_piece(g))
+            if g >= 1:
+                transpose_out(g - 1)
+            apply_gate(g)
+            if g >= 1:
+                copy_out(g - 1)
+            if g + 2 < UNIT_TILES:
+                transpose_weights(g + 2)
+            if g + 1 < LATER:
+                transpose_rows(*later_piece(g + 1))
+
+        later_steps = [(t, half) for t in range(FIRST_TILES, ROW_TILES) for half in range(UNITS // BANK)]
+        rows_step(*later_steps[0])
+        transpose_out(UNIT_TILES - 1)
+        copy_out(UNIT_TILES - 1)
+        for t, half in later_steps[1:]:
+            rows_step(t, half)

@@ -105,16 +105,11 @@ def tile_instrumentedlocmblock_pb_kernel(
         gated = {}
         flipped_out = {}
 
-        def regroup(source, grouped, passes):
-            words = source.bitcast(F32)
+        def regroup(words_of, grouped, passes):
             flipped = flip_pool.tile([P, passes * 2, P], F32, name="flipped", tag="flipped")
             for s in range(passes):
                 for u in range(2):
-                    nc.tensor.transpose(
-                        flipped[:, 2 * s + u, :],
-                        words[:, 2 * P * s + u : 2 * P * (s + 1) : 2],
-                        ident_f32[:],
-                    )
+                    nc.tensor.transpose(flipped[:, 2 * s + u, :], words_of(s, u), ident_f32[:])
             nc.scalar.copy(
                 out=grouped.bitcast(F32).rearrange("p (s r u) -> p s r u", s=passes, u=2),
                 in_=flipped[:].rearrange("p (s u) r -> p s r u", u=2),
@@ -131,20 +126,30 @@ def tile_instrumentedlocmblock_pb_kernel(
         def update_rows(t, first, count):
             ks = slice(first * K_PASS, (first + count) * K_PASS)
             y_next[t, first] = rows_pool.tile([P, count * K_PASS], BF16, name="y_next", tag="y_next")
-            nc.vector.scalar_tensor_tensor(
-                out=y_next[t, first][:],
-                in0=z_raw[:, t, ks],
-                scalar=dt_f32[:, 0:1],
-                in1=y_raw[:, t, ks],
-                op0=ALU.mult,
-                op1=ALU.add,
-            )
+            halves = y_next[t, first][:].rearrange("p (u i e) -> p u i e", u=2, e=2)
+            z_words = z_raw[:, t, ks].rearrange("p (i u e) -> p u i e", u=2, e=2)
+            y_words = y_raw[:, t, ks].rearrange("p (i u e) -> p u i e", u=2, e=2)
+            for u in range(2):
+                nc.vector.scalar_tensor_tensor(
+                    out=halves[:, u],
+                    in0=z_words[:, u],
+                    scalar=dt_f32[:, 0:1],
+                    in1=y_words[:, u],
+                    op0=ALU.mult,
+                    op1=ALU.add,
+                )
 
         def transpose_rows(t, first, count):
             y_grouped[t, first] = grouped_pool.tile(
                 [P, count * K_PASS], BF16, name="y_grouped", tag="y_grouped", align_bytes=64
             )
-            regroup(y_next[t, first][:], y_grouped[t, first][:], count)
+            words = y_next[t, first][:].bitcast(F32)
+
+            def words_of(s, u):
+                start = (u * count + s) * P
+                return words[:, start : start + P]
+
+            regroup(words_of, y_grouped[t, first][:], count)
 
         def quantise_rows(t, first, count):
             quantise(y_grouped[t, first], y_codes, y_scales, first, count, slice(t * P, (t + 1) * P))
@@ -154,7 +159,12 @@ def tile_instrumentedlocmblock_pb_kernel(
                 w_grouped[w, g] = grouped_pool.tile(
                     [P, K], BF16, name="w_grouped", tag="w_grouped", align_bytes=64
                 )
-                regroup(w_raw[w, g][:], w_grouped[w, g][:], PASSES)
+                words = w_raw[w, g][:].bitcast(F32)
+                regroup(
+                    lambda s, u: words[:, 2 * P * s + u : 2 * P * (s + 1) : 2],
+                    w_grouped[w, g][:],
+                    PASSES,
+                )
 
         def quantise_weights(g):
             for w in range(2):

@@ -58,6 +58,9 @@ def tile_instrumentedlocmblock_pb_kernel(
         table_warm = keep.tile([P, 1], F32)
         nc.scalar.activation(out=table_warm[:], in_=zero_col[:], func=ACT.Sigmoid)
 
+        filler = keep.tile([P, BANK], BF16)
+        nc.gpsimd.memset(filler[:], 0.0)
+
         dt_f32 = keep.tile([P, 1], F32)
         nc.vector.tensor_copy(out=dt_f32[:], in_=dt_bf16[:])
 
@@ -258,11 +261,18 @@ def tile_instrumentedlocmblock_pb_kernel(
             )
             nc.sync.dma_start(out=out_view[:, t, units], in_=out_rows[:, t, units])
 
+        def warm_up(count):
+            for i in range(count):
+                unread = acc_pool.tile([P, BANK], F32, name="acc_0", tag="acc_0")
+                nc.tensor.matmul(unread[:], lhsT=ident_bf16[:], rhs=filler[:], start=True, stop=True)
+
         update_rows(0, 0, PASSES)
         for t in range(FIRST_TILES):
             if t + 1 < FIRST_TILES:
                 update_rows(t + 1, 0, PASSES)
+            warm_up(4 if t == 0 else 1)
             transpose_rows(t, 0, PASSES)
+            warm_up(1)
         for t in range(FIRST_TILES):
             quantise_rows(t, 0, PASSES)
 
@@ -273,6 +283,7 @@ def tile_instrumentedlocmblock_pb_kernel(
             return FIRST_TILES + t, first, 1
 
         update_rows(*later_piece(0))
+        warm_up(1)
         transpose_weights(0)
         quantise_weights(0)
 

@@ -245,7 +245,7 @@ def tile_instrumentedlocmblock_pb_kernel(
                     out=out_view[:, 0:FIRST_TILES, units], in_=out_rows[:, 0:FIRST_TILES, units]
                 )
 
-        def rows_step(t, half):
+        def rows_step(t, half, last=False):
             units = slice(half * BANK, (half + 1) * BANK)
             sums = multiply(rows_operand(slice(t * P, (t + 1) * P)), units_operand(units))
             biased = []
@@ -255,11 +255,22 @@ def tile_instrumentedlocmblock_pb_kernel(
                     out=biased[w][:], in0=sums[w][:], in1=bias_all[:, w, units], op=ALU.add
                 )
             gate_rows = gated_pool.tile([P, BANK], F32, name="gate", tag="gate")
-            nc.scalar.activation(out=gate_rows[:], in_=biased[0][:], func=ACT.Sigmoid)
-            nc.gpsimd.tensor_tensor(
-                out=out_rows[:, t, units], in0=gate_rows[:], in1=biased[1][:], op=ALU.mult
-            )
-            nc.sync.dma_start(out=out_view[:, t, units], in_=out_rows[:, t, units])
+            pieces, multiplier = (2, nc.vector) if last else (1, nc.gpsimd)
+            width = BANK // pieces
+            parts = [slice(i * width, (i + 1) * width) for i in range(pieces)]
+            for part in parts:
+                nc.scalar.activation(
+                    out=gate_rows[:, part], in_=biased[0][:, part], func=ACT.Sigmoid
+                )
+            for part in parts:
+                stored = slice(units.start + part.start, units.start + part.stop)
+                multiplier.tensor_tensor(
+                    out=out_rows[:, t, stored],
+                    in0=gate_rows[:, part],
+                    in1=biased[1][:, part],
+                    op=ALU.mult,
+                )
+                nc.sync.dma_start(out=out_view[:, t, stored], in_=out_rows[:, t, stored])
 
         def warm_up(count):
             for i in range(count):
@@ -282,7 +293,6 @@ def tile_instrumentedlocmblock_pb_kernel(
             t, first = divmod(j, PASSES)
             return FIRST_TILES + t, first, 1
 
-        update_rows(*later_piece(0))
         warm_up(1)
         transpose_weights(0)
         quantise_weights(0)
@@ -292,29 +302,27 @@ def tile_instrumentedlocmblock_pb_kernel(
         nc.vector.tensor_copy(out=bias_cols[:], in_=bias_flipped[:, 0 : 2 * UNIT_TILES])
 
         transpose_weights(1)
-        transpose_rows(*later_piece(0))
 
         for g in range(UNIT_TILES):
             multiply_units(g)
             open_gate(g)
-            if g + 1 < LATER:
-                update_rows(*later_piece(g + 1))
+            update_rows(*later_piece(g))
             if g + 1 < UNIT_TILES:
                 quantise_weights(g + 1)
-            quantise_rows(*later_piece(g))
             if g >= 1:
+                quantise_rows(*later_piece(g - 1))
                 transpose_out(g - 1)
             apply_gate(g)
             if g >= 1:
                 copy_out(g - 1)
             if g + 2 < UNIT_TILES:
                 transpose_weights(g + 2)
-            if g + 1 < LATER:
-                transpose_rows(*later_piece(g + 1))
+            transpose_rows(*later_piece(g))
 
         later_steps = [(t, half) for t in range(FIRST_TILES, ROW_TILES) for half in range(UNITS // BANK)]
         rows_step(*later_steps[0])
         transpose_out(UNIT_TILES - 1)
         copy_out(UNIT_TILES - 1)
+        quantise_rows(*later_piece(LATER - 1))
         for t, half in later_steps[1:]:
-            rows_step(t, half)
+            rows_step(t, half, last=(t, half) == later_steps[-1])

@@ -22,7 +22,16 @@ BANK = 512
 ROW_TILES = ROWS // P
 UNIT_TILES = UNITS // P
 FIRST_TILES = BANK // P
-STORE_TILES = 2
+LATE_TILES = ROW_TILES - FIRST_TILES
+
+BIASES = 6
+UPDATE_AHEAD = 4
+QUANTISE_AFTER = 1
+APPLY_AFTER = 1
+TURN_AFTER = 5
+COPY_AFTER = 6
+OPEN_ROWS_AFTER = 1
+CLOSE_ROWS_AFTER = 3
 
 FLOPS = 2 * 2 * ROWS * K * UNITS
 
@@ -35,9 +44,10 @@ def tile_instrumentedlocmblock_pb_kernel(
         ctx.enter_context(tc.manual_schedule())
         keep = ctx.enter_context(tc.tile_pool(name="keep", bufs=1))
         rows_pool = ctx.enter_context(tc.tile_pool(name="rows", bufs=4))
-        grouped_pool = ctx.enter_context(tc.tile_pool(name="grouped", bufs=4))
-        gated_pool = ctx.enter_context(tc.tile_pool(name="gated", bufs=3))
-        acc_pool = ctx.enter_context(tc.psum_pool(name="acc", bufs=2))
+        grouped_pool = ctx.enter_context(tc.tile_pool(name="grouped", bufs=6))
+        gated_pool = ctx.enter_context(tc.tile_pool(name="gated", bufs=6))
+        biased_pool = ctx.enter_context(tc.tile_pool(name="biased", bufs=4))
+        acc_pool = ctx.enter_context(tc.psum_pool(name="acc", bufs=4))
         flip_pool = ctx.enter_context(tc.psum_pool(name="flip", bufs=4))
 
         dt_bf16 = keep.tile([P, 1], BF16)
@@ -69,69 +79,114 @@ def tile_instrumentedlocmblock_pb_kernel(
         ident_f32 = keep.tile([P, P], F32)
         make_identity(nc, ident_f32[:])
 
+        slots = [
+            ("weights", 0),
+            ("rows", 0),
+            ("warm", 1),
+            ("warm", 2),
+            ("rows", 1),
+            ("weights", 1),
+            ("warm", 1),
+            ("rows", 2),
+            ("rows", 3),
+            ("weights", 2),
+            ("multiply_units", 0, 0, 2),
+            ("multiply_units", 1, 0, 2),
+            ("rows", 4),
+            ("weights", 3),
+            ("weights", 4),
+            ("multiply_units", 0, 2, 2),
+            ("multiply_units", 1, 2, 2),
+            ("rows", 5),
+            ("multiply_units", 2, 0, FIRST_TILES),
+            ("weights", 5),
+            ("weights", 6),
+            ("multiply_units", 3, 0, FIRST_TILES),
+            ("rows", 6),
+            ("multiply_units", 4, 0, FIRST_TILES),
+            ("weights", 7),
+            ("rows", 7),
+            ("multiply_rows", 4, 0),
+            ("multiply_rows", 4, 1),
+            ("multiply_rows", 5, 0),
+            ("multiply_rows", 5, 1),
+            ("multiply_rows", 6, 0),
+            ("multiply_rows", 6, 1),
+            ("multiply_units", 5, 0, FIRST_TILES),
+            ("multiply_rows", 7, 0),
+            ("multiply_rows", 7, 1),
+            ("multiply_units", 6, 0, FIRST_TILES),
+            ("multiply_units", 7, 0, FIRST_TILES),
+        ]
+        loads = [(slot[0], slot[1]) for slot in slots if slot[0] in ("rows", "weights")]
+
         y_view = y_tilde.rearrange("(p t) k -> p t k", t=ROW_TILES)
         z_view = z_next.rearrange("(p t) k -> p t k", t=ROW_TILES)
         out_view = out.rearrange("(p t) g -> p t g", t=ROW_TILES)
         y_raw = keep.tile([P, ROW_TILES, K], BF16)
         z_raw = keep.tile([P, ROW_TILES, K], BF16)
 
+        weights = (glu_w1, glu_w2)
+        w_raw = {}
+
         def load_rows(t):
             nc.sync.dma_start(out=y_raw[:, t, :], in_=y_view[:, t, :])
             nc.sync.dma_start(out=z_raw[:, t, :], in_=z_view[:, t, :])
 
-        for t in range(FIRST_TILES):
-            load_rows(t)
-        weights = (glu_w1, glu_w2)
-        w_raw = {}
-        for g in range(UNIT_TILES):
+        def load_weights(g):
+            w_raw[g] = keep.tile([P, 2, K], BF16, name="w_raw_%d" % g)
             for w in range(2):
-                w_raw[w, g] = keep.tile([P, K], BF16, name="w_raw_%d_%d" % (w, g))
-                nc.sync.dma_start(out=w_raw[w, g][:], in_=weights[w][g * P : (g + 1) * P, :])
-            if g % 2 == 0:
-                load_rows(FIRST_TILES + g // 2)
+                nc.sync.dma_start(out=w_raw[g][:, w, :], in_=weights[w][g * P : (g + 1) * P, :])
+
+        for kind, i in loads:
+            if kind == "rows":
+                load_rows(i)
+            else:
+                load_weights(i)
         bias_all = keep.tile([P, 2, UNITS], BF16)
         nc.sync.dma_start(out=bias_all[:, 0, :], in_=glu_b1.partition_broadcast(P))
         nc.sync.dma_start(out=bias_all[:, 1, :], in_=glu_b2.partition_broadcast(P))
 
-        y_codes = keep.tile([P, PASSES, ROWS], U32, align_bytes=64)
-        y_scales = keep.tile([P, PASSES, ROWS], U8, align_bytes=64)
-        w_codes = keep.tile([P, 2, PASSES, UNITS], U32, align_bytes=64)
-        w_scales = keep.tile([P, 2, PASSES, UNITS], U8, align_bytes=64)
+        y_codes = keep.tile([P, PASSES, BANK], U32, align_bytes=64)
+        y_scales = keep.tile([P, PASSES, BANK], U8, align_bytes=64)
+        late_codes = keep.tile([P, LATE_TILES, PASSES * P], U32, align_bytes=64)
+        late_scales = keep.tile([P, LATE_TILES, PASSES * P], U8, align_bytes=64)
+        w_codes = keep.tile([P, PASSES, 2 * UNITS], U32, align_bytes=64)
+        w_scales = keep.tile([P, PASSES, 2 * UNITS], U8, align_bytes=64)
         bias_cols = keep.tile([P, 2 * UNIT_TILES], F32)
         out_rows = keep.tile([P, ROW_TILES, UNITS], F32)
 
         y_next = {}
         y_grouped = {}
         w_grouped = {}
-        acc = {}
+        sums = {}
         gate = {}
         gated = {}
         flipped_out = {}
+        row_sums = {}
+        biased = {}
+        row_gate = {}
 
-        def regroup(words_of, grouped, passes):
-            flipped = flip_pool.tile([P, passes * 2, P], F32, name="flipped", tag="flipped")
-            for s in range(passes):
+        def regroup(words_of, tag):
+            flipped = flip_pool.tile([P, 4, P], F32, name="flipped", tag="flipped")
+            for pair in range(2):
                 for u in range(2):
-                    nc.tensor.transpose(flipped[:, 2 * s + u, :], words_of(s, u), ident_f32[:])
+                    nc.tensor.transpose(flipped[:, 2 * pair + u, :], words_of(pair, u), ident_f32[:])
+            grouped = grouped_pool.tile([P, 2 * K_PASS], BF16, name=tag, tag="grouped", align_bytes=64)
             nc.scalar.copy(
-                out=grouped.bitcast(F32).rearrange("p (s r u) -> p s r u", s=passes, u=2),
-                in_=flipped[:].rearrange("p (s u) r -> p s r u", u=2),
+                out=grouped[:].bitcast(F32).rearrange("p (b r u) -> p b r u", b=2, u=2),
+                in_=flipped[:].rearrange("p (b u) r -> p b r u", u=2),
             )
+            return grouped
 
-        def quantise(grouped, codes, scales, first, count, cols):
-            for i in range(count):
-                nc.vector.quantize_mx(
-                    out=codes[:, first + i, cols].bitcast(FP8X4),
-                    scales=scales[:, first + i, cols],
-                    in_=grouped[:, i * K_PASS : (i + 1) * K_PASS],
-                )
+        def quantise(grouped, codes, scales):
+            nc.vector.quantize_mx(out=codes.bitcast(FP8X4), scales=scales, in_=grouped)
 
-        def update_rows(t, first, count):
-            ks = slice(first * K_PASS, (first + count) * K_PASS)
-            y_next[t, first] = rows_pool.tile([P, count * K_PASS], BF16, name="y_next", tag="y_next")
-            halves = y_next[t, first][:].rearrange("p (u i e) -> p u i e", u=2, e=2)
-            z_words = z_raw[:, t, ks].rearrange("p (i u e) -> p u i e", u=2, e=2)
-            y_words = y_raw[:, t, ks].rearrange("p (i u e) -> p u i e", u=2, e=2)
+        def update_rows(t):
+            y_next[t] = rows_pool.tile([P, K], BF16, name="y_next", tag="y_next")
+            halves = y_next[t][:].rearrange("p (u i e) -> p u i e", u=2, e=2)
+            z_words = z_raw[:, t, :].rearrange("p (i u e) -> p u i e", u=2, e=2)
+            y_words = y_raw[:, t, :].rearrange("p (i u e) -> p u i e", u=2, e=2)
             for u in range(2):
                 nc.vector.scalar_tensor_tensor(
                     out=halves[:, u],
@@ -142,89 +197,92 @@ def tile_instrumentedlocmblock_pb_kernel(
                     op1=ALU.add,
                 )
 
-        def transpose_rows(t, first, count):
-            y_grouped[t, first] = grouped_pool.tile(
-                [P, count * K_PASS], BF16, name="y_grouped", tag="y_grouped", align_bytes=64
+        def transpose_rows(t):
+            words = y_next[t][:].bitcast(F32)
+            y_grouped[t] = regroup(
+                lambda s, u: words[:, (PASSES * u + s) * P : (PASSES * u + s + 1) * P], "y_grouped"
             )
-            words = y_next[t, first][:].bitcast(F32)
 
-            def words_of(s, u):
-                start = (u * count + s) * P
-                return words[:, start : start + P]
-
-            regroup(words_of, y_grouped[t, first][:], count)
-
-        def quantise_rows(t, first, count):
-            quantise(y_grouped[t, first], y_codes, y_scales, first, count, slice(t * P, (t + 1) * P))
+        def quantise_rows(t):
+            grouped = y_grouped[t]
+            if t < FIRST_TILES:
+                cols = slice(t * P, (t + 1) * P)
+                for s in range(PASSES):
+                    quantise(
+                        grouped[:, s * K_PASS : (s + 1) * K_PASS],
+                        y_codes[:, s, cols],
+                        y_scales[:, s, cols],
+                    )
+            else:
+                late = t - FIRST_TILES
+                quantise(grouped[:], late_codes[:, late, :], late_scales[:, late, :])
 
         def transpose_weights(g):
-            for w in range(2):
-                w_grouped[w, g] = grouped_pool.tile(
-                    [P, K], BF16, name="w_grouped", tag="w_grouped", align_bytes=64
-                )
-                words = w_raw[w, g][:].bitcast(F32)
-                regroup(
-                    lambda s, u: words[:, 2 * P * s + u : 2 * P * (s + 1) : 2],
-                    w_grouped[w, g][:],
-                    PASSES,
+            words = w_raw[g][:].bitcast(F32)
+            for s in range(PASSES):
+                w_grouped[g, s] = regroup(
+                    lambda w, u: words[:, w, 2 * P * s + u : 2 * P * (s + 1) : 2], "w_grouped"
                 )
 
         def quantise_weights(g):
-            for w in range(2):
-                quantise(
-                    w_grouped[w, g],
-                    w_codes[:, w, :, :],
-                    w_scales[:, w, :, :],
-                    0,
-                    PASSES,
-                    slice(g * P, (g + 1) * P),
+            cols = slice(2 * g * P, 2 * (g + 1) * P)
+            for s in range(PASSES):
+                quantise(w_grouped[g, s][:], w_codes[:, s, cols], w_scales[:, s, cols])
+
+        def multiply(total, stationary, moving):
+            for s in range(PASSES):
+                lhs_codes, lhs_scales = stationary(s)
+                rhs_codes, rhs_scales = moving(s)
+                nc.tensor.matmul_mx(
+                    out=total,
+                    lhsT=lhs_codes.bitcast(FP8X4),
+                    lhsT_scale=lhs_scales,
+                    rhs=rhs_codes.bitcast(FP8X4),
+                    rhs_scale=rhs_scales,
+                    start=(s == 0),
+                    stop=(s == PASSES - 1),
                 )
 
-        def rows_operand(rows):
-            return lambda w, s: (y_codes[:, s, rows], y_scales[:, s, rows])
+        def new_bank():
+            return acc_pool.tile([P, BANK], F32, name="bank", tag="bank")
 
-        def units_operand(units):
-            return lambda w, s: (w_codes[:, w, s, units], w_scales[:, w, s, units])
+        def weights_operand(cols):
+            return lambda s: (w_codes[:, s, cols], w_scales[:, s, cols])
 
-        def multiply(stationary, moving):
-            sums = []
+        def multiply_units(g, first, count):
+            width = count * P
+            rows = slice(first * P, first * P + width)
+            banks = [new_bank() for i in range(2 * width // BANK)]
             for w in range(2):
-                total = acc_pool.tile([P, BANK], F32, name="acc_%d" % w, tag="acc_%d" % w)
-                for s in range(PASSES):
-                    lhs_codes, lhs_scales = stationary(w, s)
-                    rhs_codes, rhs_scales = moving(w, s)
-                    nc.tensor.matmul_mx(
-                        out=total[:],
-                        lhsT=lhs_codes.bitcast(FP8X4),
-                        lhsT_scale=lhs_scales,
-                        rhs=rhs_codes.bitcast(FP8X4),
-                        rhs_scale=rhs_scales,
-                        start=(s == 0),
-                        stop=(s == PASSES - 1),
-                    )
-                sums.append(total)
-            return sums
+                start = w * width % BANK
+                sums[g, first, w] = banks[w * width // BANK][:, start : start + width]
+                unit = (2 * g + w) * P
+                multiply(
+                    sums[g, first, w],
+                    weights_operand(slice(unit, unit + P)),
+                    lambda s: (y_codes[:, s, rows], y_scales[:, s, rows]),
+                )
 
-        def multiply_units(g):
-            acc[g] = multiply(units_operand(slice(g * P, (g + 1) * P)), rows_operand(slice(0, BANK)))
-
-        def open_gate(g):
-            gate[g] = gated_pool.tile([P, BANK], F32, name="gate", tag="gate")
+        def open_gate(g, first, count):
+            if g not in gate:
+                gate[g] = gated_pool.tile([P, BANK], F32, name="gate", tag="gate")
             nc.scalar.activation(
-                out=gate[g][:],
-                in_=acc[g][0][:],
+                out=gate[g][:, first * P : (first + count) * P],
+                in_=sums[g, first, 0],
                 func=ACT.Sigmoid,
                 bias=bias_cols[:, g : g + 1],
                 scale=1.0,
             )
 
-        def apply_gate(g):
-            gated[g] = gated_pool.tile([P, BANK], F32, name="gated", tag="gated")
+        def apply_gate(g, first, count):
+            rows = slice(first * P, (first + count) * P)
+            if g not in gated:
+                gated[g] = gated_pool.tile([P, BANK], F32, name="gated", tag="gated")
             nc.vector.scalar_tensor_tensor(
-                out=gated[g][:],
-                in0=acc[g][1][:],
+                out=gated[g][:, rows],
+                in0=sums[g, first, 1],
                 scalar=bias_cols[:, UNIT_TILES + g : UNIT_TILES + g + 1],
-                in1=gate[g][:],
+                in1=gate[g][:, rows],
                 op0=ALU.add,
                 op1=ALU.mult,
             )
@@ -237,92 +295,112 @@ def tile_instrumentedlocmblock_pb_kernel(
                 )
 
         def copy_out(g):
-            copy = nc.vector.tensor_copy if g % 2 == 0 else nc.scalar.copy
-            copy(out=out_rows[:, 0:FIRST_TILES, g * P : (g + 1) * P], in_=flipped_out[g][:])
-            if g % STORE_TILES == STORE_TILES - 1:
-                units = slice((g + 1 - STORE_TILES) * P, (g + 1) * P)
+            nc.scalar.copy(out=out_rows[:, 0:FIRST_TILES, g * P : (g + 1) * P], in_=flipped_out[g][:])
+            stored = 1 if g >= UNIT_TILES - 2 else 2
+            if (g + 1) % stored == 0:
+                units = slice((g + 1 - stored) * P, (g + 1) * P)
                 nc.sync.dma_start(
                     out=out_view[:, 0:FIRST_TILES, units], in_=out_rows[:, 0:FIRST_TILES, units]
                 )
 
-        def rows_step(t, half, last=False):
-            units = slice(half * BANK, (half + 1) * BANK)
-            sums = multiply(rows_operand(slice(t * P, (t + 1) * P)), units_operand(units))
-            biased = []
-            for w in range(2):
-                biased.append(gated_pool.tile([P, BANK], F32, name="biased_%d" % w, tag="biased_%d" % w))
+        HALF = UNIT_TILES // 2
+
+        def multiply_rows(t, half):
+            late = t - FIRST_TILES
+            for bank in range(2):
+                first = (2 * half + bank) * BANK
+                total = new_bank()
+                multiply(
+                    total[:],
+                    lambda s: (
+                        late_codes[:, late, s * P : (s + 1) * P],
+                        late_scales[:, late, s * P : (s + 1) * P],
+                    ),
+                    weights_operand(slice(first, first + BANK)),
+                )
+                row_sums[t, half, bank] = total
+
+        def half_units(half):
+            return slice(half * HALF * P, (half + 1) * HALF * P)
+
+        def add_biases(t, half):
+            bias = bias_all[:, :, half_units(half)].rearrange("p w (g u) -> p g w u", u=P)
+            biased[t, half] = biased_pool.tile([P, HALF, 2, P], F32, name="biased", tag="biased")
+            for bank in range(2):
+                tiles = slice(2 * bank, 2 * bank + 2)
                 nc.vector.tensor_tensor(
-                    out=biased[w][:], in0=sums[w][:], in1=bias_all[:, w, units], op=ALU.add
+                    out=biased[t, half][:, tiles],
+                    in0=row_sums[t, half, bank][:].rearrange("p (g w u) -> p g w u", g=2, w=2),
+                    in1=bias[:, tiles],
+                    op=ALU.add,
                 )
-            gate_rows = gated_pool.tile([P, BANK], F32, name="gate", tag="gate")
-            pieces, multiplier = (2, nc.vector) if last else (1, nc.gpsimd)
-            width = BANK // pieces
-            parts = [slice(i * width, (i + 1) * width) for i in range(pieces)]
-            for part in parts:
-                nc.scalar.activation(
-                    out=gate_rows[:, part], in_=biased[0][:, part], func=ACT.Sigmoid
-                )
-            for part in parts:
-                stored = slice(units.start + part.start, units.start + part.stop)
-                multiplier.tensor_tensor(
-                    out=out_rows[:, t, stored],
-                    in0=gate_rows[:, part],
-                    in1=biased[1][:, part],
-                    op=ALU.mult,
-                )
-                nc.sync.dma_start(out=out_view[:, t, stored], in_=out_rows[:, t, stored])
+
+        def open_rows(t, half):
+            row_gate[t, half] = biased_pool.tile([P, HALF, P], F32, name="row_gate", tag="row_gate")
+            nc.scalar.activation(
+                out=row_gate[t, half][:], in_=biased[t, half][:, :, 0, :], func=ACT.Sigmoid
+            )
+
+        def close_rows(t, half, engine=nc.gpsimd):
+            units = half_units(half)
+            engine.tensor_tensor(
+                out=out_rows[:, t, units].rearrange("p (g u) -> p g u", u=P),
+                in0=row_gate[t, half][:],
+                in1=biased[t, half][:, :, 1, :],
+                op=ALU.mult,
+            )
+            nc.sync.dma_start(out=out_view[:, t, units], in_=out_rows[:, t, units])
 
         def warm_up(count):
             for i in range(count):
-                unread = acc_pool.tile([P, BANK], F32, name="acc_0", tag="acc_0")
-                nc.tensor.matmul(unread[:], lhsT=ident_bf16[:], rhs=filler[:], start=True, stop=True)
+                nc.tensor.matmul(new_bank()[:], lhsT=ident_bf16[:], rhs=filler[:], start=True, stop=True)
 
-        update_rows(0, 0, PASSES)
-        for t in range(FIRST_TILES):
-            if t + 1 < FIRST_TILES:
-                update_rows(t + 1, 0, PASSES)
-            warm_up(4 if t == 0 else 1)
-            transpose_rows(t, 0, PASSES)
-            warm_up(1)
-        for t in range(FIRST_TILES):
-            quantise_rows(t, 0, PASSES)
+        due = {}
 
-        LATER = (ROW_TILES - FIRST_TILES) * PASSES
+        def plan(slot, kind, work, *what):
+            due.setdefault((max(slot, 0), kind), []).append((work, what))
 
-        def later_piece(j):
-            t, first = divmod(j, PASSES)
-            return FIRST_TILES + t, first, 1
+        row_steps = [slot[1:] for slot in slots if slot[0] == "multiply_rows"]
+        begun = set()
+        for n, slot in enumerate(slots):
+            kind, what = slot[0], slot[1:]
+            if kind == "rows":
+                plan(n - UPDATE_AHEAD, "update", update_rows, *what)
+                plan(n + QUANTISE_AFTER, "quantise", quantise_rows, *what)
+            elif kind == "weights":
+                plan(n + QUANTISE_AFTER, "quantise", quantise_weights, *what)
+            elif kind == "multiply_units":
+                g, first, count = what
+                plan(n, "gate", open_gate, *what)
+                plan(n + APPLY_AFTER, "apply", apply_gate, *what)
+                if count == FIRST_TILES or g in begun:
+                    plan(n + TURN_AFTER, "turn", transpose_out, g)
+                    plan(n + COPY_AFTER, "copy", copy_out, g)
+                begun.add(g)
+            elif kind == "multiply_rows":
+                engine = nc.vector if what == row_steps[-1] else nc.gpsimd
+                plan(n, "add", add_biases, *what)
+                plan(n + OPEN_ROWS_AFTER, "open", open_rows, *what)
+                plan(n + CLOSE_ROWS_AFTER, "close", close_rows, *what, engine)
 
-        warm_up(1)
-        transpose_weights(0)
-        quantise_weights(0)
+        products = {"multiply_units": multiply_units, "multiply_rows": multiply_rows, "warm": warm_up}
+        preparations = {"rows": transpose_rows, "weights": transpose_weights}
 
-        bias_flipped = flip_pool.tile([P, P], BF16, name="flipped", tag="flipped")
-        nc.tensor.transpose(bias_flipped[:], bias_rows[:], ident_bf16[:])
-        nc.vector.tensor_copy(out=bias_cols[:], in_=bias_flipped[:, 0 : 2 * UNIT_TILES])
+        def do(n, kinds):
+            for kind in kinds:
+                for work, what in due.get((n, kind), []):
+                    work(*what)
 
-        transpose_weights(1)
-
-        for g in range(UNIT_TILES):
-            multiply_units(g)
-            open_gate(g)
-            update_rows(*later_piece(g))
-            if g + 1 < UNIT_TILES:
-                quantise_weights(g + 1)
-            if g >= 1:
-                quantise_rows(*later_piece(g - 1))
-                transpose_out(g - 1)
-            apply_gate(g)
-            if g >= 1:
-                copy_out(g - 1)
-            if g + 2 < UNIT_TILES:
-                transpose_weights(g + 2)
-            transpose_rows(*later_piece(g))
-
-        later_steps = [(t, half) for t in range(FIRST_TILES, ROW_TILES) for half in range(UNITS // BANK)]
-        rows_step(*later_steps[0])
-        transpose_out(UNIT_TILES - 1)
-        copy_out(UNIT_TILES - 1)
-        quantise_rows(*later_piece(LATER - 1))
-        for t, half in later_steps[1:]:
-            rows_step(t, half, last=(t, half) == later_steps[-1])
+        for n in range(max(slot for slot, kind in due) + 1):
+            if n == BIASES:
+                bias_flipped = flip_pool.tile([P, P], BF16, name="flipped", tag="flipped")
+                nc.tensor.transpose(bias_flipped[:], bias_rows[:], ident_bf16[:])
+            if n == BIASES + 1:
+                nc.vector.tensor_copy(out=bias_cols[:], in_=bias_flipped[:, 0 : 2 * UNIT_TILES])
+            kind, what = (slots[n][0], slots[n][1:]) if n < len(slots) else ("none", ())
+            if kind in products:
+                products[kind](*what)
+            do(n, ("gate", "open", "close", "apply", "add", "update", "quantise", "turn"))
+            if kind in preparations:
+                preparations[kind](*what)
+            do(n, ("copy",))

@@ -24,12 +24,12 @@ UNIT_TILES = UNITS // P
 FIRST_TILES = BANK // P
 LATE_TILES = ROW_TILES - FIRST_TILES
 
-BIASES = 6
-UPDATE_AHEAD = 4
+BIASES = 12
+UPDATE_AHEAD = 7
 QUANTISE_AFTER = 1
-APPLY_AFTER = 1
-TURN_AFTER = 5
-COPY_AFTER = 6
+APPLY_AFTER = 0
+TURN_AFTER = 8
+COPY_AFTER = 8
 OPEN_ROWS_AFTER = 1
 CLOSE_ROWS_AFTER = 3
 
@@ -80,31 +80,42 @@ def tile_instrumentedlocmblock_pb_kernel(
         make_identity(nc, ident_f32[:])
 
         slots = [
-            ("weights", 0),
-            ("rows", 0),
-            ("warm", 1),
+            ("weights", 0, 0),
+            ("weights", 0, 1),
             ("warm", 2),
+            ("weights", 1, 0),
+            ("weights", 1, 1),
+            ("warm", 2),
+            ("rows", 0),
             ("rows", 1),
-            ("weights", 1),
-            ("warm", 1),
             ("rows", 2),
+            ("warm", 2),
             ("rows", 3),
-            ("weights", 2),
-            ("multiply_units", 0, 0, 2),
-            ("multiply_units", 1, 0, 2),
+            ("weights", 2, 0),
+            ("weights", 2, 1),
+            ("multiply_units", 0, 0),
+            ("multiply_units", 0, 1),
+            ("weights", 3, 0),
+            ("weights", 3, 1),
+            ("weights", 4, 0),
+            ("multiply_units", 1, 0),
+            ("multiply_units", 1, 1),
             ("rows", 4),
-            ("weights", 3),
-            ("weights", 4),
-            ("multiply_units", 0, 2, 2),
-            ("multiply_units", 1, 2, 2),
+            ("weights", 4, 1),
+            ("weights", 5, 0),
+            ("multiply_units", 2, 0),
+            ("multiply_units", 2, 1),
+            ("weights", 5, 1),
             ("rows", 5),
-            ("multiply_units", 2, 0, FIRST_TILES),
-            ("weights", 5),
-            ("weights", 6),
-            ("multiply_units", 3, 0, FIRST_TILES),
+            ("weights", 6, 0),
+            ("multiply_units", 3, 0),
+            ("multiply_units", 3, 1),
+            ("weights", 6, 1),
             ("rows", 6),
-            ("multiply_units", 4, 0, FIRST_TILES),
-            ("weights", 7),
+            ("weights", 7, 0),
+            ("multiply_units", 4, 0),
+            ("multiply_units", 4, 1),
+            ("weights", 7, 1),
             ("rows", 7),
             ("multiply_rows", 4, 0),
             ("multiply_rows", 4, 1),
@@ -112,13 +123,15 @@ def tile_instrumentedlocmblock_pb_kernel(
             ("multiply_rows", 5, 1),
             ("multiply_rows", 6, 0),
             ("multiply_rows", 6, 1),
-            ("multiply_units", 5, 0, FIRST_TILES),
             ("multiply_rows", 7, 0),
             ("multiply_rows", 7, 1),
-            ("multiply_units", 6, 0, FIRST_TILES),
-            ("multiply_units", 7, 0, FIRST_TILES),
+            ("multiply_units", 5, 0),
+            ("multiply_units", 5, 1),
+            ("multiply_units", 6, 0),
+            ("multiply_units", 6, 1),
+            ("multiply_units", 7, 0),
+            ("multiply_units", 7, 1),
         ]
-        loads = [(slot[0], slot[1]) for slot in slots if slot[0] in ("rows", "weights")]
 
         y_view = y_tilde.rearrange("(p t) k -> p t k", t=ROW_TILES)
         z_view = z_next.rearrange("(p t) k -> p t k", t=ROW_TILES)
@@ -138,11 +151,11 @@ def tile_instrumentedlocmblock_pb_kernel(
             for w in range(2):
                 nc.sync.dma_start(out=w_raw[g][:, w, :], in_=weights[w][g * P : (g + 1) * P, :])
 
-        for kind, i in loads:
-            if kind == "rows":
-                load_rows(i)
-            else:
-                load_weights(i)
+        for slot in slots:
+            if slot[0] == "rows":
+                load_rows(slot[1])
+            elif slot[0] == "weights" and slot[1] not in w_raw:
+                load_weights(slot[1])
         bias_all = keep.tile([P, 2, UNITS], BF16)
         nc.sync.dma_start(out=bias_all[:, 0, :], in_=glu_b1.partition_broadcast(P))
         nc.sync.dma_start(out=bias_all[:, 1, :], in_=glu_b2.partition_broadcast(P))
@@ -217,17 +230,15 @@ def tile_instrumentedlocmblock_pb_kernel(
                 late = t - FIRST_TILES
                 quantise(grouped[:], late_codes[:, late, :], late_scales[:, late, :])
 
-        def transpose_weights(g):
+        def transpose_weights(g, s):
             words = w_raw[g][:].bitcast(F32)
-            for s in range(PASSES):
-                w_grouped[g, s] = regroup(
-                    lambda w, u: words[:, w, 2 * P * s + u : 2 * P * (s + 1) : 2], "w_grouped"
-                )
+            w_grouped[g, s] = regroup(
+                lambda w, u: words[:, w, 2 * P * s + u : 2 * P * (s + 1) : 2], "w_grouped"
+            )
 
-        def quantise_weights(g):
+        def quantise_weights(g, s):
             cols = slice(2 * g * P, 2 * (g + 1) * P)
-            for s in range(PASSES):
-                quantise(w_grouped[g, s][:], w_codes[:, s, cols], w_scales[:, s, cols])
+            quantise(w_grouped[g, s][:], w_codes[:, s, cols], w_scales[:, s, cols])
 
         def multiply(total, stationary, moving):
             for s in range(PASSES):
@@ -249,40 +260,32 @@ def tile_instrumentedlocmblock_pb_kernel(
         def weights_operand(cols):
             return lambda s: (w_codes[:, s, cols], w_scales[:, s, cols])
 
-        def multiply_units(g, first, count):
-            width = count * P
-            rows = slice(first * P, first * P + width)
-            banks = [new_bank() for i in range(2 * width // BANK)]
-            for w in range(2):
-                start = w * width % BANK
-                sums[g, first, w] = banks[w * width // BANK][:, start : start + width]
-                unit = (2 * g + w) * P
-                multiply(
-                    sums[g, first, w],
-                    weights_operand(slice(unit, unit + P)),
-                    lambda s: (y_codes[:, s, rows], y_scales[:, s, rows]),
-                )
+        def multiply_units(g, w):
+            sums[g, w] = new_bank()
+            unit = (2 * g + w) * P
+            multiply(
+                sums[g, w][:],
+                weights_operand(slice(unit, unit + P)),
+                lambda s: (y_codes[:, s, :], y_scales[:, s, :]),
+            )
 
-        def open_gate(g, first, count):
-            if g not in gate:
-                gate[g] = gated_pool.tile([P, BANK], F32, name="gate", tag="gate")
+        def open_gate(g):
+            gate[g] = gated_pool.tile([P, BANK], F32, name="gate", tag="gate")
             nc.scalar.activation(
-                out=gate[g][:, first * P : (first + count) * P],
-                in_=sums[g, first, 0],
+                out=gate[g][:],
+                in_=sums[g, 0][:],
                 func=ACT.Sigmoid,
                 bias=bias_cols[:, g : g + 1],
                 scale=1.0,
             )
 
-        def apply_gate(g, first, count):
-            rows = slice(first * P, (first + count) * P)
-            if g not in gated:
-                gated[g] = gated_pool.tile([P, BANK], F32, name="gated", tag="gated")
+        def apply_gate(g):
+            gated[g] = gated_pool.tile([P, BANK], F32, name="gated", tag="gated")
             nc.vector.scalar_tensor_tensor(
-                out=gated[g][:, rows],
-                in0=sums[g, first, 1],
+                out=gated[g][:],
+                in0=sums[g, 1][:],
                 scalar=bias_cols[:, UNIT_TILES + g : UNIT_TILES + g + 1],
-                in1=gate[g][:, rows],
+                in1=gate[g][:],
                 op0=ALU.add,
                 op1=ALU.mult,
             )
@@ -361,7 +364,6 @@ def tile_instrumentedlocmblock_pb_kernel(
             due.setdefault((max(slot, 0), kind), []).append((work, what))
 
         row_steps = [slot[1:] for slot in slots if slot[0] == "multiply_rows"]
-        begun = set()
         for n, slot in enumerate(slots):
             kind, what = slot[0], slot[1:]
             if kind == "rows":
@@ -370,13 +372,13 @@ def tile_instrumentedlocmblock_pb_kernel(
             elif kind == "weights":
                 plan(n + QUANTISE_AFTER, "quantise", quantise_weights, *what)
             elif kind == "multiply_units":
-                g, first, count = what
-                plan(n, "gate", open_gate, *what)
-                plan(n + APPLY_AFTER, "apply", apply_gate, *what)
-                if count == FIRST_TILES or g in begun:
+                g, w = what
+                if w == 0:
+                    plan(n, "gate", open_gate, g)
+                else:
+                    plan(n + APPLY_AFTER, "apply", apply_gate, g)
                     plan(n + TURN_AFTER, "turn", transpose_out, g)
                     plan(n + COPY_AFTER, "copy", copy_out, g)
-                begun.add(g)
             elif kind == "multiply_rows":
                 engine = nc.vector if what == row_steps[-1] else nc.gpsimd
                 plan(n, "add", add_biases, *what)

@@ -24,7 +24,7 @@ UNIT_TILES = UNITS // P
 FIRST_TILES = BANK // P
 LATE_TILES = ROW_TILES - FIRST_TILES
 
-BIASES = 12
+BIASES = 15
 UPDATE_AHEAD = 7
 QUANTISE_AFTER = 1
 APPLY_AFTER = 0
@@ -80,17 +80,21 @@ def tile_instrumentedlocmblock_pb_kernel(
         make_identity(nc, ident_f32[:])
 
         slots = [
+            ("warm", 4),
             ("weights", 0, 0),
             ("weights", 0, 1),
-            ("warm", 2),
+            ("warm", 3),
             ("weights", 1, 0),
             ("weights", 1, 1),
-            ("warm", 2),
+            ("warm", 3),
             ("rows", 0),
+            ("warm", 1),
             ("rows", 1),
+            ("warm", 1),
             ("rows", 2),
             ("warm", 2),
             ("rows", 3),
+            ("warm", 2),
             ("weights", 2, 0),
             ("weights", 2, 1),
             ("multiply_units", 0, 0),

@@ -24,8 +24,8 @@ UNIT_TILES = UNITS // P
 FIRST_TILES = BANK // P
 LATE_TILES = ROW_TILES - FIRST_TILES
 
-BIASES = 15
-UPDATE_AHEAD = 7
+BIASES = 12
+UPDATE_AHEAD = 6
 QUANTISE_AFTER = 1
 APPLY_AFTER = 0
 TURN_AFTER = 8
@@ -81,20 +81,19 @@ def tile_instrumentedlocmblock_pb_kernel(
 
         slots = [
             ("warm", 4),
-            ("weights", 0, 0),
-            ("weights", 0, 1),
-            ("warm", 3),
-            ("weights", 1, 0),
-            ("weights", 1, 1),
-            ("warm", 3),
             ("rows", 0),
-            ("warm", 1),
+            ("warm", 2),
             ("rows", 1),
-            ("warm", 1),
+            ("warm", 2),
             ("rows", 2),
             ("warm", 2),
+            ("weights", 0, 0),
+            ("weights", 0, 1),
+            ("warm", 1),
             ("rows", 3),
-            ("warm", 2),
+            ("warm", 1),
+            ("weights", 1, 0),
+            ("weights", 1, 1),
             ("weights", 2, 0),
             ("weights", 2, 1),
             ("multiply_units", 0, 0),
@@ -104,8 +103,8 @@ def tile_instrumentedlocmblock_pb_kernel(
             ("weights", 4, 0),
             ("multiply_units", 1, 0),
             ("multiply_units", 1, 1),
-            ("rows", 4),
             ("weights", 4, 1),
+            ("rows", 4),
             ("weights", 5, 0),
             ("multiply_units", 2, 0),
             ("multiply_units", 2, 1),
@@ -115,8 +114,8 @@ def tile_instrumentedlocmblock_pb_kernel(
             ("multiply_units", 3, 0),
             ("multiply_units", 3, 1),
             ("weights", 6, 1),
-            ("rows", 6),
             ("weights", 7, 0),
+            ("rows", 6),
             ("multiply_units", 4, 0),
             ("multiply_units", 4, 1),
             ("weights", 7, 1),
@@ -128,9 +127,9 @@ def tile_instrumentedlocmblock_pb_kernel(
             ("multiply_rows", 6, 0),
             ("multiply_rows", 6, 1),
             ("multiply_rows", 7, 0),
-            ("multiply_rows", 7, 1),
             ("multiply_units", 5, 0),
             ("multiply_units", 5, 1),
+            ("multiply_rows", 7, 1),
             ("multiply_units", 6, 0),
             ("multiply_units", 6, 1),
             ("multiply_units", 7, 0),
@@ -302,8 +301,9 @@ def tile_instrumentedlocmblock_pb_kernel(
                 )
 
         def copy_out(g):
-            nc.scalar.copy(out=out_rows[:, 0:FIRST_TILES, g * P : (g + 1) * P], in_=flipped_out[g][:])
-            stored = 1 if g >= UNIT_TILES - 2 else 2
+            copy = nc.vector.tensor_copy if g == UNIT_TILES - 2 else nc.scalar.copy
+            copy(out=out_rows[:, 0:FIRST_TILES, g * P : (g + 1) * P], in_=flipped_out[g][:])
+            stored = 1 if g >= UNIT_TILES // 2 else 2
             if (g + 1) % stored == 0:
                 units = slice((g + 1 - stored) * P, (g + 1) * P)
                 nc.sync.dma_start(

@@ -91,11 +91,13 @@ def tile_instrumentedlocmblock_pb_kernel(
             ("weights", 0, 1),
             ("warm", 1),
             ("rows", 3),
-            ("warm", 1),
+            ("warm", 2),
             ("weights", 1, 0),
             ("weights", 1, 1),
+            ("warm", 1),
             ("weights", 2, 0),
             ("weights", 2, 1),
+            ("warm", 1),
             ("multiply_units", 0, 0),
             ("multiply_units", 0, 1),
             ("weights", 3, 0),
@@ -145,9 +147,15 @@ def tile_instrumentedlocmblock_pb_kernel(
         weights = (glu_w1, glu_w2)
         w_raw = {}
 
+        def row_pieces(t):
+            if t == FIRST_TILES - 1:
+                return [slice(s * K_PASS, (s + 1) * K_PASS) for s in range(PASSES)]
+            return [slice(0, K)]
+
         def load_rows(t):
-            nc.sync.dma_start(out=y_raw[:, t, :], in_=y_view[:, t, :])
-            nc.sync.dma_start(out=z_raw[:, t, :], in_=z_view[:, t, :])
+            for ks in row_pieces(t):
+                nc.sync.dma_start(out=y_raw[:, t, ks], in_=y_view[:, t, ks])
+                nc.sync.dma_start(out=z_raw[:, t, ks], in_=z_view[:, t, ks])
 
         def load_weights(g):
             w_raw[g] = keep.tile([P, 2, K], BF16, name="w_raw_%d" % g)
@@ -200,18 +208,20 @@ def tile_instrumentedlocmblock_pb_kernel(
 
         def update_rows(t):
             y_next[t] = rows_pool.tile([P, K], BF16, name="y_next", tag="y_next")
-            halves = y_next[t][:].rearrange("p (u i e) -> p u i e", u=2, e=2)
-            z_words = z_raw[:, t, :].rearrange("p (i u e) -> p u i e", u=2, e=2)
-            y_words = y_raw[:, t, :].rearrange("p (i u e) -> p u i e", u=2, e=2)
-            for u in range(2):
-                nc.vector.scalar_tensor_tensor(
-                    out=halves[:, u],
-                    in0=z_words[:, u],
-                    scalar=dt_f32[:, 0:1],
-                    in1=y_words[:, u],
-                    op0=ALU.mult,
-                    op1=ALU.add,
-                )
+            halves = y_next[t][:].rearrange("p (u k) -> p u k", u=2)
+            for ks in row_pieces(t):
+                half = halves[:, :, ks.start // 2 : ks.stop // 2]
+                z_words = z_raw[:, t, ks].rearrange("p (i u e) -> p u i e", u=2, e=2)
+                y_words = y_raw[:, t, ks].rearrange("p (i u e) -> p u i e", u=2, e=2)
+                for u in range(2):
+                    nc.vector.scalar_tensor_tensor(
+                        out=half[:, u].rearrange("p (i e) -> p i e", e=2),
+                        in0=z_words[:, u],
+                        scalar=dt_f32[:, 0:1],
+                        in1=y_words[:, u],
+                        op0=ALU.mult,
+                        op1=ALU.add,
+                    )
 
         def transpose_rows(t):
             words = y_next[t][:].bitcast(F32)
@@ -282,33 +292,43 @@ def tile_instrumentedlocmblock_pb_kernel(
                 scale=1.0,
             )
 
+        def row_parts(g):
+            count = FIRST_TILES // 2 if g == UNIT_TILES - 1 else FIRST_TILES
+            return [(first, count) for first in range(0, FIRST_TILES, count)]
+
         def apply_gate(g):
             gated[g] = gated_pool.tile([P, BANK], F32, name="gated", tag="gated")
-            nc.vector.scalar_tensor_tensor(
-                out=gated[g][:],
-                in0=sums[g, 1][:],
-                scalar=bias_cols[:, UNIT_TILES + g : UNIT_TILES + g + 1],
-                in1=gate[g][:],
-                op0=ALU.add,
-                op1=ALU.mult,
-            )
+            for first, count in row_parts(g):
+                rows = slice(first * P, (first + count) * P)
+                nc.vector.scalar_tensor_tensor(
+                    out=gated[g][:, rows],
+                    in0=sums[g, 1][:, rows],
+                    scalar=bias_cols[:, UNIT_TILES + g : UNIT_TILES + g + 1],
+                    in1=gate[g][:, rows],
+                    op0=ALU.add,
+                    op1=ALU.mult,
+                )
 
         def transpose_out(g):
-            flipped_out[g] = flip_pool.tile([P, FIRST_TILES, P], F32, name="flipped", tag="flipped")
-            for t in range(FIRST_TILES):
-                nc.tensor.transpose(
-                    flipped_out[g][:, t, :], gated[g][:, t * P : (t + 1) * P], ident_f32[:]
-                )
+            for first, count in row_parts(g):
+                flipped = flip_pool.tile([P, count, P], F32, name="flipped", tag="flipped")
+                for i in range(count):
+                    rows = slice((first + i) * P, (first + i + 1) * P)
+                    nc.tensor.transpose(flipped[:, i, :], gated[g][:, rows], ident_f32[:])
+                flipped_out[g, first] = flipped
 
         def copy_out(g):
-            copy = nc.vector.tensor_copy if g == UNIT_TILES - 2 else nc.scalar.copy
-            copy(out=out_rows[:, 0:FIRST_TILES, g * P : (g + 1) * P], in_=flipped_out[g][:])
-            stored = 1 if g >= UNIT_TILES // 2 else 2
-            if (g + 1) % stored == 0:
-                units = slice((g + 1 - stored) * P, (g + 1) * P)
-                nc.sync.dma_start(
-                    out=out_view[:, 0:FIRST_TILES, units], in_=out_rows[:, 0:FIRST_TILES, units]
-                )
+            for first, count in row_parts(g):
+                on_vector = g == UNIT_TILES - 2 or first > 0
+                copy = nc.vector.tensor_copy if on_vector else nc.scalar.copy
+                tiles = slice(first, first + count)
+                copy(out=out_rows[:, tiles, g * P : (g + 1) * P], in_=flipped_out[g, first][:])
+                stored = 1 if g >= UNIT_TILES // 2 else 2
+                if (g + 1) % stored == 0:
+                    units = slice((g + 1 - stored) * P, (g + 1) * P)
+                    nc.sync.dma_start(
+                        out=out_view[:, tiles, units], in_=out_rows[:, tiles, units]
+                    )
 
         HALF = UNIT_TILES // 2
 
@@ -348,7 +368,7 @@ def tile_instrumentedlocmblock_pb_kernel(
                 out=row_gate[t, half][:], in_=biased[t, half][:, :, 0, :], func=ACT.Sigmoid
             )
 
-        def close_rows(t, half, engine=nc.gpsimd):
+        def close_rows(t, half, engine):
             units = half_units(half)
             engine.tensor_tensor(
                 out=out_rows[:, t, units].rearrange("p (g u) -> p g u", u=P),
@@ -367,7 +387,7 @@ def tile_instrumentedlocmblock_pb_kernel(
         def plan(slot, kind, work, *what):
             due.setdefault((max(slot, 0), kind), []).append((work, what))
 
-        row_steps = [slot[1:] for slot in slots if slot[0] == "multiply_rows"]
+        last_rows = [slot[1:] for slot in slots if slot[0] == "multiply_rows"][-1]
         for n, slot in enumerate(slots):
             kind, what = slot[0], slot[1:]
             if kind == "rows":
@@ -384,9 +404,9 @@ def tile_instrumentedlocmblock_pb_kernel(
                     plan(n + TURN_AFTER, "turn", transpose_out, g)
                     plan(n + COPY_AFTER, "copy", copy_out, g)
             elif kind == "multiply_rows":
-                engine = nc.vector if what == row_steps[-1] else nc.gpsimd
                 plan(n, "add", add_biases, *what)
                 plan(n + OPEN_ROWS_AFTER, "open", open_rows, *what)
+                engine = nc.vector if what == last_rows else nc.gpsimd
                 plan(n + CLOSE_ROWS_AFTER, "close", close_rows, *what, engine)
 
         products = {"multiply_units": multiply_units, "multiply_rows": multiply_rows, "warm": warm_up}

from contextlib import ExitStack

import concourse.mybir as mybir
from concourse.masks import make_identity

F32 = mybir.dt.float32
BF16 = mybir.dt.bfloat16
U32 = mybir.dt.uint32
U8 = mybir.dt.uint8
FP8X4 = mybir.dt.float8_e4m3fn_x4
ALU = mybir.AluOpType
ACT = mybir.ActivationFunctionType

P = 128
ROWS = 1024
K = 1024
UNITS = 1024
PACK = 4
K_PASS = P * PACK
PASSES = K // K_PASS
BANK = 512
ROW_TILES = ROWS // P
UNIT_TILES = UNITS // P
FIRST_TILES = BANK // P
LATE_TILES = ROW_TILES - FIRST_TILES

BIASES = 12
UPDATE_AHEAD = 6
QUANTISE_AFTER = 1
APPLY_AFTER = 0
TURN_AFTER = 8
COPY_AFTER = 8
OPEN_ROWS_AFTER = 1
CLOSE_ROWS_AFTER = 3

FLOPS = 2 * 2 * ROWS * K * UNITS


def tile_instrumentedlocmblock_pb_kernel(
    tc, y_tilde, z_next, dt, glu_w1, glu_w2, glu_b1, glu_b2, out
):
    nc = tc.nc
    with ExitStack() as ctx:
        ctx.enter_context(tc.manual_schedule())
        keep = ctx.enter_context(tc.tile_pool(name="keep", bufs=1))
        rows_pool = ctx.enter_context(tc.tile_pool(name="rows", bufs=4))
        grouped_pool = ctx.enter_context(tc.tile_pool(name="grouped", bufs=6))
        gated_pool = ctx.enter_context(tc.tile_pool(name="gated", bufs=6))
        biased_pool = ctx.enter_context(tc.tile_pool(name="biased", bufs=4))
        acc_pool = ctx.enter_context(tc.psum_pool(name="acc", bufs=4))
        flip_pool = ctx.enter_context(tc.psum_pool(name="flip", bufs=4))

        dt_bf16 = keep.tile([P, 1], BF16)
        nc.scalar.dma_start(out=dt_bf16[:], in_=dt.partition_broadcast(P))

        bias_rows = keep.tile([P, P], BF16)
        nc.vector.memset(bias_rows[:], 0.0)
        nc.scalar.dma_start(
            out=bias_rows[0:UNIT_TILES, :], in_=glu_b1.rearrange("(g p) -> g p", p=P)
        )
        nc.scalar.dma_start(
            out=bias_rows[UNIT_TILES : 2 * UNIT_TILES, :],
            in_=glu_b2.rearrange("(g p) -> g p", p=P),
        )

        zero_col = keep.tile([P, 1], F32)
        nc.vector.memset(zero_col[:], 0.0)
        table_warm = keep.tile([P, 1], F32)
        nc.scalar.activation(out=table_warm[:], in_=zero_col[:], func=ACT.Sigmoid)

        filler = keep.tile([P, BANK], BF16)
        nc.gpsimd.memset(filler[:], 0.0)

        dt_f32 = keep.tile([P, 1], F32)
        nc.vector.tensor_copy(out=dt_f32[:], in_=dt_bf16[:])

        ident_bf16 = keep.tile([P, P], BF16)
        make_identity(nc, ident_bf16[:])
        ident_f32 = keep.tile([P, P], F32)
        make_identity(nc, ident_f32[:])

        slots = [
            ("warm", 4),
            ("rows", 0),
            ("warm", 2),
            ("rows", 1),
            ("warm", 2),
            ("rows", 2),
            ("warm", 2),
            ("weights", 0, 0),
            ("weights", 0, 1),
            ("warm", 1),
            ("rows", 3),
            ("warm", 2),
            ("weights", 1, 0),
            ("weights", 1, 1),
            ("warm", 1),
            ("weights", 2, 0),
            ("weights", 2, 1),
            ("warm", 1),
            ("multiply_units", 0, 0),
            ("multiply_units", 0, 1),
            ("weights", 3, 0),
            ("weights", 3, 1),
            ("weights", 4, 0),
            ("multiply_units", 1, 0),
            ("multiply_units", 1, 1),
            ("weights", 4, 1),
            ("rows", 4),
            ("weights", 5, 0),
            ("multiply_units", 2, 0),
            ("multiply_units", 2, 1),
            ("weights", 5, 1),
            ("rows", 5),
            ("weights", 6, 0),
            ("multiply_units", 3, 0),
            ("multiply_units", 3, 1),
            ("weights", 6, 1),
            ("weights", 7, 0),
            ("rows", 6),
            ("multiply_units", 4, 0),
            ("multiply_units", 4, 1),
            ("weights", 7, 1),
            ("rows", 7),
            ("multiply_rows", 4, 0),
            ("multiply_rows", 4, 1),
            ("multiply_rows", 5, 0),
            ("multiply_rows", 5, 1),
            ("multiply_rows", 6, 0),
            ("multiply_rows", 6, 1),
            ("multiply_rows", 7, 0),
            ("multiply_units", 5, 0),
            ("multiply_units", 5, 1),
            ("multiply_rows", 7, 1),
            ("multiply_units", 6, 0),
            ("multiply_units", 6, 1),
            ("multiply_units", 7, 0),
            ("multiply_units", 7, 1),
        ]

        y_view = y_tilde.rearrange("(p t) k -> p t k", t=ROW_TILES)
        z_view = z_next.rearrange("(p t) k -> p t k", t=ROW_TILES)
        out_view = out.rearrange("(p t) g -> p t g", t=ROW_TILES)
        y_raw = keep.tile([P, ROW_TILES, K], BF16)
        z_raw = keep.tile([P, ROW_TILES, K], BF16)

        weights = (glu_w1, glu_w2)
        w_raw = {}

        def row_pieces(t):
            if t == FIRST_TILES - 1:
                return [slice(s * K_PASS, (s + 1) * K_PASS) for s in range(PASSES)]
            return [slice(0, K)]

        def load_rows(t):
            for ks in row_pieces(t):
                nc.sync.dma_start(out=y_raw[:, t, ks], in_=y_view[:, t, ks])
                nc.sync.dma_start(out=z_raw[:, t, ks], in_=z_view[:, t, ks])

        def load_weights(g):
            w_raw[g] = keep.tile([P, 2, K], BF16, name="w_raw_%d" % g)
            for w in range(2):
                nc.sync.dma_start(out=w_raw[g][:, w, :], in_=weights[w][g * P : (g + 1) * P, :])

        for slot in slots:
            if slot[0] == "rows":
                load_rows(slot[1])
            elif slot[0] == "weights" and slot[1] not in w_raw:
                load_weights(slot[1])
        bias_all = keep.tile([P, 2, UNITS], BF16)
        nc.sync.dma_start(out=bias_all[:, 0, :], in_=glu_b1.partition_broadcast(P))
        nc.sync.dma_start(out=bias_all[:, 1, :], in_=glu_b2.partition_broadcast(P))

        y_codes = keep.tile([P, PASSES, BANK], U32, align_bytes=64)
        y_scales = keep.tile([P, PASSES, BANK], U8, align_bytes=64)
        late_codes = keep.tile([P, LATE_TILES, PASSES * P], U32, align_bytes=64)
        late_scales = keep.tile([P, LATE_TILES, PASSES * P], U8, align_bytes=64)
        w_codes = keep.tile([P, PASSES, 2 * UNITS], U32, align_bytes=64)
        w_scales = keep.tile([P, PASSES, 2 * UNITS], U8, align_bytes=64)
        bias_cols = keep.tile([P, 2 * UNIT_TILES], F32)
        out_rows = keep.tile([P, ROW_TILES, UNITS], F32)

        y_next = {}
        y_grouped = {}
        w_grouped = {}
        sums = {}
        gate = {}
        gated = {}
        flipped_out = {}
        row_sums = {}
        biased = {}
        row_gate = {}

        def regroup(words_of, tag):
            flipped = flip_pool.tile([P, 4, P], F32, name="flipped", tag="flipped")
            for pair in range(2):
                for u in range(2):
                    nc.tensor.transpose(flipped[:, 2 * pair + u, :], words_of(pair, u), ident_f32[:])
            grouped = grouped_pool.tile([P, 2 * K_PASS], BF16, name=tag, tag="grouped", align_bytes=64)
            nc.scalar.copy(
                out=grouped[:].bitcast(F32).rearrange("p (b r u) -> p b r u", b=2, u=2),
                in_=flipped[:].rearrange("p (b u) r -> p b r u", u=2),
            )
            return grouped

        def quantise(grouped, codes, scales):
            nc.vector.quantize_mx(out=codes.bitcast(FP8X4), scales=scales, in_=grouped)

        def update_rows(t):
            y_next[t] = rows_pool.tile([P, K], BF16, name="y_next", tag="y_next")
            halves = y_next[t][:].rearrange("p (u k) -> p u k", u=2)
            for ks in row_pieces(t):
                half = halves[:, :, ks.start // 2 : ks.stop // 2]
                z_words = z_raw[:, t, ks].rearrange("p (i u e) -> p u i e", u=2, e=2)
                y_words = y_raw[:, t, ks].rearrange("p (i u e) -> p u i e", u=2, e=2)
                for u in range(2):
                    nc.vector.scalar_tensor_tensor(
                        out=half[:, u].rearrange("p (i e) -> p i e", e=2),
                        in0=z_words[:, u],
                        scalar=dt_f32[:, 0:1],
                        in1=y_words[:, u],
                        op0=ALU.mult,
                        op1=ALU.add,
                    )

        def transpose_rows(t):
            words = y_next[t][:].bitcast(F32)
            y_grouped[t] = regroup(
                lambda s, u: words[:, (PASSES * u + s) * P : (PASSES * u + s + 1) * P], "y_grouped"
            )

        def quantise_rows(t):
            grouped = y_grouped[t]
            if t < FIRST_TILES:
                cols = slice(t * P, (t + 1) * P)
                for s in range(PASSES):
                    quantise(
                        grouped[:, s * K_PASS : (s + 1) * K_PASS],
                        y_codes[:, s, cols],
                        y_scales[:, s, cols],
                    )
            else:
                late = t - FIRST_TILES
                quantise(grouped[:], late_codes[:, late, :], late_scales[:, late, :])

        def transpose_weights(g, s):
            words = w_raw[g][:].bitcast(F32)
            w_grouped[g, s] = regroup(
                lambda w, u: words[:, w, 2 * P * s + u : 2 * P * (s + 1) : 2], "w_grouped"
            )

        def quantise_weights(g, s):
            cols = slice(2 * g * P, 2 * (g + 1) * P)
            quantise(w_grouped[g, s][:], w_codes[:, s, cols], w_scales[:, s, cols])

        def multiply(total, stationary, moving):
            for s in range(PASSES):
                lhs_codes, lhs_scales = stationary(s)
                rhs_codes, rhs_scales = moving(s)
                nc.tensor.matmul_mx(
                    out=total,
                    lhsT=lhs_codes.bitcast(FP8X4),
                    lhsT_scale=lhs_scales,
                    rhs=rhs_codes.bitcast(FP8X4),
                    rhs_scale=rhs_scales,
                    start=(s == 0),
                    stop=(s == PASSES - 1),
                )

        def new_bank():
            return acc_pool.tile([P, BANK], F32, name="bank", tag="bank")

        def weights_operand(cols):
            return lambda s: (w_codes[:, s, cols], w_scales[:, s, cols])

        def multiply_units(g, w):
            sums[g, w] = new_bank()
            unit = (2 * g + w) * P
            multiply(
                sums[g, w][:],
                weights_operand(slice(unit, unit + P)),
                lambda s: (y_codes[:, s, :], y_scales[:, s, :]),
            )

        def open_gate(g):
            gate[g] = gated_pool.tile([P, BANK], F32, name="gate", tag="gate")
            nc.scalar.activation(
                out=gate[g][:],
                in_=sums[g, 0][:],
                func=ACT.Sigmoid,
                bias=bias_cols[:, g : g + 1],
                scale=1.0,
            )

        def row_parts(g):
            count = FIRST_TILES // 2 if g == UNIT_TILES - 1 else FIRST_TILES
            return [(first, count) for first in range(0, FIRST_TILES, count)]

        def apply_gate(g):
            gated[g] = gated_pool.tile([P, BANK], F32, name="gated", tag="gated")
            for first, count in row_parts(g):
                rows = slice(first * P, (first + count) * P)
                nc.vector.scalar_tensor_tensor(
                    out=gated[g][:, rows],
                    in0=sums[g, 1][:, rows],
                    scalar=bias_cols[:, UNIT_TILES + g : UNIT_TILES + g + 1],
                    in1=gate[g][:, rows],
                    op0=ALU.add,
                    op1=ALU.mult,
                )

        def transpose_out(g):
            for first, count in row_parts(g):
                flipped = flip_pool.tile([P, count, P], F32, name="flipped", tag="flipped")
                for i in range(count):
                    rows = slice((first + i) * P, (first + i + 1) * P)
                    nc.tensor.transpose(flipped[:, i, :], gated[g][:, rows], ident_f32[:])
                flipped_out[g, first] = flipped

        def copy_out(g):
            for first, count in row_parts(g):
                on_vector = g == UNIT_TILES - 2 or first > 0
                copy = nc.vector.tensor_copy if on_vector else nc.scalar.copy
                tiles = slice(first, first + count)
                copy(out=out_rows[:, tiles, g * P : (g + 1) * P], in_=flipped_out[g, first][:])
                stored = 1 if g >= UNIT_TILES // 2 else 2
                if (g + 1) % stored == 0:
                    units = slice((g + 1 - stored) * P, (g + 1) * P)
                    nc.sync.dma_start(
                        out=out_view[:, tiles, units], in_=out_rows[:, tiles, units]
                    )

        HALF = UNIT_TILES // 2

        def multiply_rows(t, half):
            late = t - FIRST_TILES
            for bank in range(2):
                first = (2 * half + bank) * BANK
                total = new_bank()
                multiply(
                    total[:],
                    lambda s: (
                        late_codes[:, late, s * P : (s + 1) * P],
                        late_scales[:, late, s * P : (s + 1) * P],
                    ),
                    weights_operand(slice(first, first + BANK)),
                )
                row_sums[t, half, bank] = total

        def half_units(half):
            return slice(half * HALF * P, (half + 1) * HALF * P)

        def add_biases(t, half):
            bias = bias_all[:, :, half_units(half)].rearrange("p w (g u) -> p g w u", u=P)
            biased[t, half] = biased_pool.tile([P, HALF, 2, P], F32, name="biased", tag="biased")
            for bank in range(2):
                tiles = slice(2 * bank, 2 * bank + 2)
                nc.vector.tensor_tensor(
                    out=biased[t, half][:, tiles],
                    in0=row_sums[t, half, bank][:].rearrange("p (g w u) -> p g w u", g=2, w=2),
                    in1=bias[:, tiles],
                    op=ALU.add,
                )

        def open_rows(t, half):
            row_gate[t, half] = biased_pool.tile([P, HALF, P], F32, name="row_gate", tag="row_gate")
            nc.scalar.activation(
                out=row_gate[t, half][:], in_=biased[t, half][:, :, 0, :], func=ACT.Sigmoid
            )

        def close_rows(t, half, engine):
            units = half_units(half)
            engine.tensor_tensor(
                out=out_rows[:, t, units].rearrange("p (g u) -> p g u", u=P),
                in0=row_gate[t, half][:],
                in1=biased[t, half][:, :, 1, :],
                op=ALU.mult,
            )
            nc.sync.dma_start(out=out_view[:, t, units], in_=out_rows[:, t, units])

        def warm_up(count):
            for i in range(count):
                nc.tensor.matmul(new_bank()[:], lhsT=ident_bf16[:], rhs=filler[:], start=True, stop=True)

        due = {}

        def plan(slot, kind, work, *what):
            due.setdefault((max(slot, 0), kind), []).append((work, what))

        last_rows = [slot[1:] for slot in slots if slot[0] == "multiply_rows"][-1]
        for n, slot in enumerate(slots):
            kind, what = slot[0], slot[1:]
            if kind == "rows":
                plan(n - UPDATE_AHEAD, "update", update_rows, *what)
                plan(n + QUANTISE_AFTER, "quantise", quantise_rows, *what)
            elif kind == "weights":
                plan(n + QUANTISE_AFTER, "quantise", quantise_weights, *what)
            elif kind == "multiply_units":
                g, w = what
                if w == 0:
                    plan(n, "gate", open_gate, g)
                else:
                    plan(n + APPLY_AFTER, "apply", apply_gate, g)
                    plan(n + TURN_AFTER, "turn", transpose_out, g)
                    plan(n + COPY_AFTER, "copy", copy_out, g)
            elif kind == "multiply_rows":
                plan(n, "add", add_biases, *what)
                plan(n + OPEN_ROWS_AFTER, "open", open_rows, *what)
                engine = nc.vector if what == last_rows else nc.gpsimd
                plan(n + CLOSE_ROWS_AFTER, "close", close_rows, *what, engine)

        products = {"multiply_units": multiply_units, "multiply_rows": multiply_rows, "warm": warm_up}
        preparations = {"rows": transpose_rows, "weights": transpose_weights}

        def do(n, kinds):
            for kind in kinds:
                for work, what in due.get((n, kind), []):
                    work(*what)

        for n in range(max(slot for slot, kind in due) + 1):
            if n == BIASES:
                bias_flipped = flip_pool.tile([P, P], BF16, name="flipped", tag="flipped")
                nc.tensor.transpose(bias_flipped[:], bias_rows[:], ident_bf16[:])
            if n == BIASES + 1:
                nc.vector.tensor_copy(out=bias_cols[:], in_=bias_flipped[:, 0 : 2 * UNIT_TILES])
            kind, what = (slots[n][0], slots[n][1:]) if n < len(slots) else ("none", ())
            if kind in products:
                products[kind](*what)
            do(n, ("gate", "open", "close", "apply", "add", "update", "quantise", "turn"))
            if kind in preparations:
                preparations[kind](*what)
            do(n, ("copy",))
